import numpy as np
import ml_dtypes

BF16 = ml_dtypes.bfloat16


def bf(x):
    return np.asarray(x, np.float32).astype(BF16)


def f32(x):
    return np.asarray(x, np.float32)


def f64(x):
    return np.asarray(x).astype(np.float64)


def striped(idx):
    return np.tile(idx.reshape(-1, 16).T, (8, 1))


D, H, C, S, N = 512, 256, 256, 4096, 2048


def setup_inputs():
    return {
        "base": f32(np.random.standard_normal((C, S)) / np.sqrt(C)),
        "y1": bf(np.random.standard_normal((D, N))),
        "w_enc": bf(np.random.standard_normal((D, H)) / np.sqrt(D)),
        "w_proj": bf(0.5 * np.random.standard_normal((H, C)) / np.sqrt(H)),
        "offs": striped(np.random.permutation(S)[:N]),
    }


def reference(base, y1, w_enc, w_proj, offs):
    idx = offs[:16].T.reshape(-1)
    h = f64(w_enc).T @ f64(y1)
    z = f64(w_proj).T @ h
    r = 1.0 / np.sqrt(np.sum(z * z, axis=0, keepdims=True))
    out = f64(base).copy()
    out[:, idx] = z * r
    return out

@@ -1,0 +1,90 @@
+import concourse.mybir as mybir
+
+F32 = mybir.dt.float32
+BF16 = mybir.dt.bfloat16
+U16 = mybir.dt.uint16
+FUNC = mybir.ActivationFunctionType
+MULT = mybir.AluOpType.mult
+
+P = 128
+D, H, C, S, N = 512, 256, 256, 4096, 2048
+BANK = 512
+PSUM_BANKS = 8
+D_BLOCKS, H_BLOCKS, C_BLOCKS, N_BLOCKS = D // P, H // P, C // P, N // BANK
+
+FLOPS = 2 * N * (D * H + H * C + C)
+
+
+def tile_momentumcontrast_s_kernel(tc, base, y1, w_enc, w_proj, offs, out):
+    nc = tc.nc
+    with (
+        tc.tile_pool(name="held", bufs=1) as held,
+        tc.tile_pool(name="blocks", bufs=N_BLOCKS) as blocks,
+        tc.psum_pool(name="psum", bufs=PSUM_BANKS) as psum,
+    ):
+        offsets = held.tile([P, N // 16], U16, name="offsets")
+        w_enc_sb = held.tile([P, D_BLOCKS, H], BF16, name="w_enc_sb")
+        w_proj_sb = held.tile([P, H_BLOCKS, C], BF16, name="w_proj_sb")
+        y_sb = [held.tile([P, D_BLOCKS, BANK], BF16, name=f"y{q}") for q in range(N_BLOCKS)]
+        window = [held.tile([P, S], F32, name=f"window{c}") for c in range(C_BLOCKS)]
+        z_sb = [held.tile([P, N], F32, name=f"z{c}") for c in range(C_BLOCKS)]
+        r_sb = held.tile([P, N], F32, name="r_sb")
+        ones = held.tile([P, P], F32, name="ones")
+
+        nc.sync.dma_start(offsets[:], offs)
+        y_view = y1.rearrange("(k p) n -> p k n", p=P)
+        loads = [(w_enc_sb[:], w_enc.rearrange("(k p) i -> p k i", p=P))]
+        loads += [(y_sb[0][:], y_view[:, :, 0:BANK])]
+        loads += [(w_proj_sb[:], w_proj.rearrange("(k p) c -> p k c", p=P))]
+        loads += [(y_sb[q][:], y_view[:, :, q * BANK : (q + 1) * BANK]) for q in range(1, N_BLOCKS)]
+        loads += [(window[c][:], base[c * P : (c + 1) * P, :]) for c in range(C_BLOCKS)]
+        for turn, (tile, source) in enumerate(loads):
+            queue = nc.sync if turn % 2 == 0 else nc.scalar
+            queue.dma_start(tile, source)
+
+        nc.vector.memset(ones[:], 1.0)
+
+        h_sb = []
+        for q in range(N_BLOCKS):
+            h_sb.append(blocks.tile([P, H_BLOCKS, BANK], BF16, name="h_sb"))
+            for i in range(H_BLOCKS):
+                h_ps = psum.tile([P, BANK], F32, tag="bank")
+                for k in range(D_BLOCKS):
+                    nc.tensor.matmul(
+                        h_ps[:],
+                        w_enc_sb[:, k, i * P : (i + 1) * P],
+                        y_sb[q][:, k, :],
+                        start=(k == 0),
+                        stop=(k == D_BLOCKS - 1),
+                    )
+                nc.vector.tensor_copy(h_sb[q][:, i, :], h_ps[:])
+
+        squares = []
+        for q in range(N_BLOCKS):
+            columns = slice(q * BANK, (q + 1) * BANK)
+            squares.append(blocks.tile([P, C_BLOCKS, BANK], F32, name="squares"))
+            for c in range(C_BLOCKS):
+                z_ps = psum.tile([P, BANK], F32, tag="bank")
+                for i in range(H_BLOCKS):
+                    nc.tensor.matmul(
+                        z_ps[:],
+                        w_proj_sb[:, i, c * P : (c + 1) * P],
+                        h_sb[q][:, i, :],
+                        start=(i == 0),
+                        stop=(i == H_BLOCKS - 1),
+                    )
+                nc.vector.tensor_copy(z_sb[c][:, columns], z_ps[:])
+                nc.scalar.activation(squares[q][:, c, :], z_ps[:], FUNC.Square)
+
+        for q in range(N_BLOCKS):
+            columns = slice(q * BANK, (q + 1) * BANK)
+            sum_ps = psum.tile([P, BANK], F32, tag="bank")
+            for c in range(C_BLOCKS):
+                nc.tensor.matmul(
+                    sum_ps[:], ones[:], squares[q][:, c, :], start=(c == 0), stop=(c == C_BLOCKS - 1)
+                )
+            nc.scalar.activation(r_sb[:, columns], sum_ps[:], FUNC.Abs_reciprocal_sqrt)
+
+        for c in range(C_BLOCKS):
+            nc.vector.tensor_tensor(window[c][:].indirect(offsets[:]), z_sb[c][:], r_sb[:], MULT)
+            nc.sync.dma_start(out[c * P : (c + 1) * P, :], window[c][:])

@@ -11,6 +11,9 @@ D, H, C, S, N = 512, 256, 256, 4096, 2048
 BANK = 512
 PSUM_BANKS = 8
 D_BLOCKS, H_BLOCKS, C_BLOCKS, N_BLOCKS = D // P, H // P, C // P, N // BANK
+HALVES = 2
+HALF = N // HALVES
+HALF_BLOCKS = HALF // BANK
 
 FLOPS = 2 * N * (D * H + H * C + C)
 
@@ -19,6 +22,7 @@ def tile_momentumcontrast_s_kernel(tc, base, y1, w_enc, w_proj, offs, out):
     nc = tc.nc
     with (
         tc.tile_pool(name="held", bufs=1) as held,
+        tc.tile_pool(name="halves", bufs=HALVES) as halves,
         tc.tile_pool(name="blocks", bufs=N_BLOCKS) as blocks,
         tc.psum_pool(name="psum", bufs=PSUM_BANKS) as psum,
     ):
@@ -27,64 +31,73 @@ def tile_momentumcontrast_s_kernel(tc, base, y1, w_enc, w_proj, offs, out):
         w_proj_sb = held.tile([P, H_BLOCKS, C], BF16, name="w_proj_sb")
         y_sb = [held.tile([P, D_BLOCKS, BANK], BF16, name=f"y{q}") for q in range(N_BLOCKS)]
         window = [held.tile([P, S], F32, name=f"window{c}") for c in range(C_BLOCKS)]
-        z_sb = [held.tile([P, N], F32, name=f"z{c}") for c in range(C_BLOCKS)]
-        r_sb = held.tile([P, N], F32, name="r_sb")
         ones = held.tile([P, P], F32, name="ones")
 
         nc.sync.dma_start(offsets[:], offs)
         y_view = y1.rearrange("(k p) n -> p k n", p=P)
         loads = [(w_enc_sb[:], w_enc.rearrange("(k p) i -> p k i", p=P))]
         loads += [(y_sb[0][:], y_view[:, :, 0:BANK])]
+        loads += [(y_sb[1][:], y_view[:, :, BANK : 2 * BANK])]
         loads += [(w_proj_sb[:], w_proj.rearrange("(k p) c -> p k c", p=P))]
-        loads += [(y_sb[q][:], y_view[:, :, q * BANK : (q + 1) * BANK]) for q in range(1, N_BLOCKS)]
-        loads += [(window[c][:], base[c * P : (c + 1) * P, :]) for c in range(C_BLOCKS)]
+        loads += [(y_sb[q][:], y_view[:, :, q * BANK : (q + 1) * BANK]) for q in range(2, N_BLOCKS)]
+        for c in range(C_BLOCKS):
+            for slots in (slice(0, S // 2), slice(S // 2, S)):
+                loads += [(window[c][:, slots], base[c * P : (c + 1) * P, slots])]
         for turn, (tile, source) in enumerate(loads):
             queue = nc.sync if turn % 2 == 0 else nc.scalar
             queue.dma_start(tile, source)
 
         nc.vector.memset(ones[:], 1.0)
 
-        h_sb = []
-        for q in range(N_BLOCKS):
-            h_sb.append(blocks.tile([P, H_BLOCKS, BANK], BF16, name="h_sb"))
-            for i in range(H_BLOCKS):
-                h_ps = psum.tile([P, BANK], F32, tag="bank")
-                for k in range(D_BLOCKS):
-                    nc.tensor.matmul(
-                        h_ps[:],
-                        w_enc_sb[:, k, i * P : (i + 1) * P],
-                        y_sb[q][:, k, :],
-                        start=(k == 0),
-                        stop=(k == D_BLOCKS - 1),
-                    )
-                nc.vector.tensor_copy(h_sb[q][:, i, :], h_ps[:])
+        for half in range(HALVES):
+            copy_out = nc.vector.tensor_copy if half == 0 else nc.scalar.copy
+            z_sb = [halves.tile([P, HALF], F32, name=f"z{c}") for c in range(C_BLOCKS)]
+            r_sb = halves.tile([P, HALF], F32, name="r_sb")
 
-        squares = []
-        for q in range(N_BLOCKS):
-            columns = slice(q * BANK, (q + 1) * BANK)
-            squares.append(blocks.tile([P, C_BLOCKS, BANK], F32, name="squares"))
-            for c in range(C_BLOCKS):
-                z_ps = psum.tile([P, BANK], F32, tag="bank")
+            h_sb = []
+            for b in range(HALF_BLOCKS):
+                h_sb.append(blocks.tile([P, H_BLOCKS, BANK], BF16, name="h_sb"))
                 for i in range(H_BLOCKS):
-                    nc.tensor.matmul(
-                        z_ps[:],
-                        w_proj_sb[:, i, c * P : (c + 1) * P],
-                        h_sb[q][:, i, :],
-                        start=(i == 0),
-                        stop=(i == H_BLOCKS - 1),
-                    )
-                nc.vector.tensor_copy(z_sb[c][:, columns], z_ps[:])
-                nc.scalar.activation(squares[q][:, c, :], z_ps[:], FUNC.Square)
+                    h_ps = psum.tile([P, BANK], F32, tag="bank")
+                    for k in range(D_BLOCKS):
+                        nc.tensor.matmul(
+                            h_ps[:],
+                            w_enc_sb[:, k, i * P : (i + 1) * P],
+                            y_sb[half * HALF_BLOCKS + b][:, k, :],
+                            start=(k == 0),
+                            stop=(k == D_BLOCKS - 1),
+                        )
+                    copy_out(h_sb[b][:, i, :], h_ps[:])
 
-        for q in range(N_BLOCKS):
-            columns = slice(q * BANK, (q + 1) * BANK)
-            sum_ps = psum.tile([P, BANK], F32, tag="bank")
-            for c in range(C_BLOCKS):
-                nc.tensor.matmul(
-                    sum_ps[:], ones[:], squares[q][:, c, :], start=(c == 0), stop=(c == C_BLOCKS - 1)
+            squares = []
+            for b in range(HALF_BLOCKS):
+                squares.append(blocks.tile([P, C_BLOCKS, BANK], F32, name="squares"))
+                for c in range(C_BLOCKS):
+                    z_ps = psum.tile([P, BANK], F32, tag="bank")
+                    for i in range(H_BLOCKS):
+                        nc.tensor.matmul(
+                            z_ps[:],
+                            w_proj_sb[:, i, c * P : (c + 1) * P],
+                            h_sb[b][:, i, :],
+                            start=(i == 0),
+                            stop=(i == H_BLOCKS - 1),
+                        )
+                    nc.scalar.activation(squares[b][:, c, :], z_ps[:], FUNC.Square)
+                    copy_out(z_sb[c][:, b * BANK : (b + 1) * BANK], z_ps[:])
+
+            for b in range(HALF_BLOCKS):
+                sum_ps = psum.tile([P, BANK], F32, tag="bank")
+                for c in range(C_BLOCKS):
+                    nc.tensor.matmul(
+                        sum_ps[:], ones[:], squares[b][:, c, :], start=(c == 0), stop=(c == C_BLOCKS - 1)
+                    )
+                nc.scalar.activation(
+                    r_sb[:, b * BANK : (b + 1) * BANK], sum_ps[:], FUNC.Abs_reciprocal_sqrt
                 )
-            nc.scalar.activation(r_sb[:, columns], sum_ps[:], FUNC.Abs_reciprocal_sqrt)
+
+            listed = offsets[:, half * (HALF // 16) : (half + 1) * (HALF // 16)]
+            for c in range(C_BLOCKS):
+                nc.vector.tensor_tensor(window[c][:].indirect(listed), z_sb[c][:], r_sb[:], MULT)
 
         for c in range(C_BLOCKS):
-            nc.vector.tensor_tensor(window[c][:].indirect(offsets[:]), z_sb[c][:], r_sb[:], MULT)
             nc.sync.dma_start(out[c * P : (c + 1) * P, :], window[c][:])

@@ -14,6 +14,7 @@ D_BLOCKS, H_BLOCKS, C_BLOCKS, N_BLOCKS = D // P, H // P, C // P, N // BANK
 HALVES = 2
 HALF = N // HALVES
 HALF_BLOCKS = HALF // BANK
+WARM_UP_MATMULS = 5
 
 FLOPS = 2 * N * (D * H + H * C + C)
 
@@ -35,8 +36,10 @@ def tile_momentumcontrast_s_kernel(tc, base, y1, w_enc, w_proj, offs, out):
 
         nc.sync.dma_start(offsets[:], offs)
         y_view = y1.rearrange("(k p) n -> p k n", p=P)
-        loads = [(w_enc_sb[:], w_enc.rearrange("(k p) i -> p k i", p=P))]
-        loads += [(y_sb[0][:], y_view[:, :, 0:BANK])]
+        w_enc_view = w_enc.rearrange("(k p) i -> p k i", p=P)
+        loads = []
+        for k in range(D_BLOCKS):
+            loads += [(w_enc_sb[:, k, :], w_enc_view[:, k, :]), (y_sb[0][:, k, :], y_view[:, k, 0:BANK])]
         loads += [(y_sb[1][:], y_view[:, :, BANK : 2 * BANK])]
         loads += [(w_proj_sb[:], w_proj.rearrange("(k p) c -> p k c", p=P))]
         loads += [(y_sb[q][:], y_view[:, :, q * BANK : (q + 1) * BANK]) for q in range(2, N_BLOCKS)]
@@ -48,6 +51,12 @@ def tile_momentumcontrast_s_kernel(tc, base, y1, w_enc, w_proj, offs, out):
             queue.dma_start(tile, source)
 
         nc.vector.memset(ones[:], 1.0)
+
+        zeros = held.tile([P, BANK], BF16, name="zeros")
+        nc.vector.memset(zeros[:], 0.0)
+        unread_ps = psum.tile([P, BANK], F32, tag="bank")
+        for repeat in range(WARM_UP_MATMULS):
+            nc.tensor.matmul(unread_ps[:], zeros[:, 0:P], zeros[:], start=True, stop=True)
 
         for half in range(HALVES):
             copy_out = nc.vector.tensor_copy if half == 0 else nc.scalar.copy

@@ -14,7 +14,6 @@ D_BLOCKS, H_BLOCKS, C_BLOCKS, N_BLOCKS = D // P, H // P, C // P, N // BANK
 HALVES = 2
 HALF = N // HALVES
 HALF_BLOCKS = HALF // BANK
-WARM_UP_MATMULS = 5
 
 FLOPS = 2 * N * (D * H + H * C + C)
 
@@ -51,12 +50,6 @@ def tile_momentumcontrast_s_kernel(tc, base, y1, w_enc, w_proj, offs, out):
             queue.dma_start(tile, source)
 
         nc.vector.memset(ones[:], 1.0)
-
-        zeros = held.tile([P, BANK], BF16, name="zeros")
-        nc.vector.memset(zeros[:], 0.0)
-        unread_ps = psum.tile([P, BANK], F32, tag="bank")
-        for repeat in range(WARM_UP_MATMULS):
-            nc.tensor.matmul(unread_ps[:], zeros[:, 0:P], zeros[:], start=True, stop=True)
 
         for half in range(HALVES):
             copy_out = nc.vector.tensor_copy if half == 0 else nc.scalar.copy

@@ -11,9 +11,7 @@ D, H, C, S, N = 512, 256, 256, 4096, 2048
 BANK = 512
 PSUM_BANKS = 8
 D_BLOCKS, H_BLOCKS, C_BLOCKS, N_BLOCKS = D // P, H // P, C // P, N // BANK
-HALVES = 2
-HALF = N // HALVES
-HALF_BLOCKS = HALF // BANK
+LIST_COLUMNS = BANK // 16
 
 FLOPS = 2 * N * (D * H + H * C + C)
 
@@ -22,7 +20,6 @@ def tile_momentumcontrast_s_kernel(tc, base, y1, w_enc, w_proj, offs, out):
     nc = tc.nc
     with (
         tc.tile_pool(name="held", bufs=1) as held,
-        tc.tile_pool(name="halves", bufs=HALVES) as halves,
         tc.tile_pool(name="blocks", bufs=N_BLOCKS) as blocks,
         tc.psum_pool(name="psum", bufs=PSUM_BANKS) as psum,
     ):
@@ -33,73 +30,83 @@ def tile_momentumcontrast_s_kernel(tc, base, y1, w_enc, w_proj, offs, out):
         window = [held.tile([P, S], F32, name=f"window{c}") for c in range(C_BLOCKS)]
         ones = held.tile([P, P], F32, name="ones")
 
-        nc.sync.dma_start(offsets[:], offs)
         y_view = y1.rearrange("(k p) n -> p k n", p=P)
-        w_enc_view = w_enc.rearrange("(k p) i -> p k i", p=P)
-        loads = []
-        for k in range(D_BLOCKS):
-            loads += [(w_enc_sb[:, k, :], w_enc_view[:, k, :]), (y_sb[0][:, k, :], y_view[:, k, 0:BANK])]
-        loads += [(y_sb[1][:], y_view[:, :, BANK : 2 * BANK])]
-        loads += [(w_proj_sb[:], w_proj.rearrange("(k p) c -> p k c", p=P))]
-        loads += [(y_sb[q][:], y_view[:, :, q * BANK : (q + 1) * BANK]) for q in range(2, N_BLOCKS)]
-        for c in range(C_BLOCKS):
-            for slots in (slice(0, S // 2), slice(S // 2, S)):
-                loads += [(window[c][:, slots], base[c * P : (c + 1) * P, slots])]
-        for turn, (tile, source) in enumerate(loads):
-            queue = nc.sync if turn % 2 == 0 else nc.scalar
-            queue.dma_start(tile, source)
+        k_half = D_BLOCKS // 2
+        nc.sync.dma_start(w_enc_sb[:], w_enc.rearrange("(k p) i -> p k i", p=P))
+        nc.scalar.dma_start(y_sb[0][:, 0:k_half, :], y_view[:, 0:k_half, 0:BANK])
+        nc.sync.dma_start(y_sb[0][:, k_half:D_BLOCKS, :], y_view[:, k_half:D_BLOCKS, 0:BANK])
+        nc.scalar.dma_start(w_proj_sb[:], w_proj.rearrange("(k p) c -> p k c", p=P))
+        nc.sync.dma_start(y_sb[1][:], y_view[:, :, BANK : 2 * BANK])
+        nc.sync.dma_start(window[0][:, 0 : S // 2], base[0:P, 0 : S // 2])
+        nc.scalar.dma_start(window[0][:, S // 2 : S], base[0:P, S // 2 : S])
+        nc.sync.dma_start(offsets[:], offs)
+        nc.sync.dma_start(window[1][:], base[P : 2 * P, :])
+        for q in range(2, N_BLOCKS):
+            nc.sync.dma_start(y_sb[q][:], y_view[:, :, q * BANK : (q + 1) * BANK])
 
         nc.vector.memset(ones[:], 1.0)
 
-        for half in range(HALVES):
-            copy_out = nc.vector.tensor_copy if half == 0 else nc.scalar.copy
-            z_sb = [halves.tile([P, HALF], F32, name=f"z{c}") for c in range(C_BLOCKS)]
-            r_sb = halves.tile([P, HALF], F32, name="r_sb")
+        h_sb = [held.tile([P, H_BLOCKS, BANK], BF16, name=f"h{q}") for q in range(N_BLOCKS)]
+        z_sb = [[held.tile([P, BANK], F32, name=f"z{q}_{c}") for c in range(C_BLOCKS)] for q in range(N_BLOCKS)]
+        r_sb = [held.tile([P, BANK], F32, name=f"r{q}") for q in range(N_BLOCKS)]
+        z_ps = {}
+        squares = {}
 
-            h_sb = []
-            for b in range(HALF_BLOCKS):
-                h_sb.append(blocks.tile([P, H_BLOCKS, BANK], BF16, name="h_sb"))
-                for i in range(H_BLOCKS):
-                    h_ps = psum.tile([P, BANK], F32, tag="bank")
-                    for k in range(D_BLOCKS):
-                        nc.tensor.matmul(
-                            h_ps[:],
-                            w_enc_sb[:, k, i * P : (i + 1) * P],
-                            y_sb[half * HALF_BLOCKS + b][:, k, :],
-                            start=(k == 0),
-                            stop=(k == D_BLOCKS - 1),
-                        )
-                    copy_out(h_sb[b][:, i, :], h_ps[:])
+        def second_copier(q):
+            return nc.vector.tensor_copy if q == 0 else nc.scalar.copy
 
-            squares = []
-            for b in range(HALF_BLOCKS):
-                squares.append(blocks.tile([P, C_BLOCKS, BANK], F32, name="squares"))
-                for c in range(C_BLOCKS):
-                    z_ps = psum.tile([P, BANK], F32, tag="bank")
-                    for i in range(H_BLOCKS):
-                        nc.tensor.matmul(
-                            z_ps[:],
-                            w_proj_sb[:, i, c * P : (c + 1) * P],
-                            h_sb[b][:, i, :],
-                            start=(i == 0),
-                            stop=(i == H_BLOCKS - 1),
-                        )
-                    nc.scalar.activation(squares[b][:, c, :], z_ps[:], FUNC.Square)
-                    copy_out(z_sb[c][:, b * BANK : (b + 1) * BANK], z_ps[:])
+        def encode(q, hidden_blocks):
+            h_ps = {i: psum.tile([P, BANK], F32, tag="bank", name=f"h_ps{i}") for i in hidden_blocks}
+            for k in range(D_BLOCKS):
+                for i in hidden_blocks:
+                    nc.tensor.matmul(
+                        h_ps[i][:],
+                        w_enc_sb[:, k, i * P : (i + 1) * P],
+                        y_sb[q][:, k, :],
+                        start=(k == 0),
+                        stop=(k == D_BLOCKS - 1),
+                    )
+            for i in hidden_blocks:
+                copy_out = nc.scalar.copy if i == 0 else second_copier(q)
+                copy_out(h_sb[q][:, i, :], h_ps[i][:])
 
-            for b in range(HALF_BLOCKS):
-                sum_ps = psum.tile([P, BANK], F32, tag="bank")
+        def project(q):
+            z_ps[q] = [psum.tile([P, BANK], F32, tag="bank", name=f"z_ps{c}") for c in range(C_BLOCKS)]
+            for i in range(H_BLOCKS):
                 for c in range(C_BLOCKS):
                     nc.tensor.matmul(
-                        sum_ps[:], ones[:], squares[b][:, c, :], start=(c == 0), stop=(c == C_BLOCKS - 1)
+                        z_ps[q][c][:],
+                        w_proj_sb[:, i, c * P : (c + 1) * P],
+                        h_sb[q][:, i, :],
+                        start=(i == 0),
+                        stop=(i == H_BLOCKS - 1),
                     )
-                nc.scalar.activation(
-                    r_sb[:, b * BANK : (b + 1) * BANK], sum_ps[:], FUNC.Abs_reciprocal_sqrt
-                )
-
-            listed = offsets[:, half * (HALF // 16) : (half + 1) * (HALF // 16)]
+            squares[q] = blocks.tile([P, C_BLOCKS, BANK], F32, name="squares")
             for c in range(C_BLOCKS):
-                nc.vector.tensor_tensor(window[c][:].indirect(listed), z_sb[c][:], r_sb[:], MULT)
+                nc.scalar.activation(squares[q][:, c, :], z_ps[q][c][:], FUNC.Square)
+
+        def norm(q):
+            sum_ps = psum.tile([P, BANK], F32, tag="bank")
+            for c in range(C_BLOCKS):
+                nc.tensor.matmul(sum_ps[:], ones[:], squares[q][:, c, :], start=(c == 0), stop=(c == C_BLOCKS - 1))
+            second_copier(q)(z_sb[q][0][:], z_ps[q][0][:])
+            nc.scalar.activation(r_sb[q][:], sum_ps[:], FUNC.Abs_reciprocal_sqrt)
+            second_copier(q)(z_sb[q][1][:], z_ps[q][1][:])
+
+        def place(q):
+            listed = offsets[:, q * LIST_COLUMNS : (q + 1) * LIST_COLUMNS]
+            for c in range(C_BLOCKS):
+                nc.vector.tensor_tensor(window[c][:].indirect(listed), z_sb[q][c][:], r_sb[q][:], MULT)
+
+        encode(0, (0, 1))
+        for q in range(N_BLOCKS):
+            project(q)
+            if q + 1 < N_BLOCKS:
+                encode(q + 1, (0,))
+            norm(q)
+            if q + 1 < N_BLOCKS:
+                encode(q + 1, (1,))
+            place(q)
 
         for c in range(C_BLOCKS):
             nc.sync.dma_start(out[c * P : (c + 1) * P, :], window[c][:])

@@ -8,10 +8,13 @@ MULT = mybir.AluOpType.mult
 
 P = 128
 D, H, C, S, N = 512, 256, 256, 4096, 2048
-BANK = 512
+D_BLOCKS, H_BLOCKS, C_BLOCKS = D // P, H // P, C // P
+PIECE = 512
+PIECES = N // PIECE
+STEPS = 2
+STEP = PIECE // STEPS
+LIST_COLUMNS = PIECE // 16
 PSUM_BANKS = 8
-D_BLOCKS, H_BLOCKS, C_BLOCKS, N_BLOCKS = D // P, H // P, C // P, N // BANK
-LIST_COLUMNS = BANK // 16
 
 FLOPS = 2 * N * (D * H + H * C + C)
 
@@ -20,93 +23,80 @@ def tile_momentumcontrast_s_kernel(tc, base, y1, w_enc, w_proj, offs, out):
     nc = tc.nc
     with (
         tc.tile_pool(name="held", bufs=1) as held,
-        tc.tile_pool(name="blocks", bufs=N_BLOCKS) as blocks,
+        tc.tile_pool(name="ring", bufs=2 * STEPS) as ring,
         tc.psum_pool(name="psum", bufs=PSUM_BANKS) as psum,
     ):
         offsets = held.tile([P, N // 16], U16, name="offsets")
         w_enc_sb = held.tile([P, D_BLOCKS, H], BF16, name="w_enc_sb")
         w_proj_sb = held.tile([P, H_BLOCKS, C], BF16, name="w_proj_sb")
-        y_sb = [held.tile([P, D_BLOCKS, BANK], BF16, name=f"y{q}") for q in range(N_BLOCKS)]
         window = [held.tile([P, S], F32, name=f"window{c}") for c in range(C_BLOCKS)]
         ones = held.tile([P, P], F32, name="ones")
+        y_sb = [held.tile([P, D_BLOCKS, PIECE], BF16, name=f"y{q}") for q in range(PIECES)]
+        h_sb = [held.tile([P, H_BLOCKS, PIECE], BF16, name=f"h{q}") for q in range(PIECES)]
+        z_sb = [[held.tile([P, PIECE], F32, name=f"z{q}_{c}") for c in range(C_BLOCKS)] for q in range(PIECES)]
+        r_sb = [held.tile([P, PIECE], F32, name=f"r{q}") for q in range(PIECES)]
 
         y_view = y1.rearrange("(k p) n -> p k n", p=P)
-        k_half = D_BLOCKS // 2
         nc.sync.dma_start(w_enc_sb[:], w_enc.rearrange("(k p) i -> p k i", p=P))
-        nc.scalar.dma_start(y_sb[0][:, 0:k_half, :], y_view[:, 0:k_half, 0:BANK])
-        nc.sync.dma_start(y_sb[0][:, k_half:D_BLOCKS, :], y_view[:, k_half:D_BLOCKS, 0:BANK])
+        nc.scalar.dma_start(y_sb[0][:, :, 0:STEP], y_view[:, :, 0:STEP])
+        nc.sync.dma_start(y_sb[0][:, :, STEP:PIECE], y_view[:, :, STEP:PIECE])
         nc.scalar.dma_start(w_proj_sb[:], w_proj.rearrange("(k p) c -> p k c", p=P))
-        nc.sync.dma_start(y_sb[1][:], y_view[:, :, BANK : 2 * BANK])
-        nc.sync.dma_start(window[0][:, 0 : S // 2], base[0:P, 0 : S // 2])
-        nc.scalar.dma_start(window[0][:, S // 2 : S], base[0:P, S // 2 : S])
+        nc.sync.dma_start(y_sb[1][:], y_view[:, :, PIECE : 2 * PIECE])
+        nc.sync.dma_start(window[0][:], base[0:P, :])
         nc.sync.dma_start(offsets[:], offs)
         nc.sync.dma_start(window[1][:], base[P : 2 * P, :])
-        for q in range(2, N_BLOCKS):
-            nc.sync.dma_start(y_sb[q][:], y_view[:, :, q * BANK : (q + 1) * BANK])
+        for q in range(2, PIECES):
+            nc.sync.dma_start(y_sb[q][:], y_view[:, :, q * PIECE : (q + 1) * PIECE])
 
         nc.vector.memset(ones[:], 1.0)
 
-        h_sb = [held.tile([P, H_BLOCKS, BANK], BF16, name=f"h{q}") for q in range(N_BLOCKS)]
-        z_sb = [[held.tile([P, BANK], F32, name=f"z{q}_{c}") for c in range(C_BLOCKS)] for q in range(N_BLOCKS)]
-        r_sb = [held.tile([P, BANK], F32, name=f"r{q}") for q in range(N_BLOCKS)]
-        z_ps = {}
-        squares = {}
+        for q in range(PIECES):
+            second_copier = nc.vector.tensor_copy if q == 0 else nc.scalar.copy
+            columns = [slice(s * STEP, (s + 1) * STEP) for s in range(STEPS)]
 
-        def second_copier(q):
-            return nc.vector.tensor_copy if q == 0 else nc.scalar.copy
+            for s in range(STEPS):
+                for i in range(H_BLOCKS):
+                    h_ps = psum.tile([P, STEP], F32, tag="bank")
+                    for k in range(D_BLOCKS):
+                        nc.tensor.matmul(
+                            h_ps[:],
+                            w_enc_sb[:, k, i * P : (i + 1) * P],
+                            y_sb[q][:, k, columns[s]],
+                            start=(k == 0),
+                            stop=(k == D_BLOCKS - 1),
+                        )
+                    copy_out = nc.scalar.copy if i == 0 else second_copier
+                    copy_out(h_sb[q][:, i, columns[s]], h_ps[:])
 
-        def encode(q, hidden_blocks):
-            h_ps = {i: psum.tile([P, BANK], F32, tag="bank", name=f"h_ps{i}") for i in hidden_blocks}
-            for k in range(D_BLOCKS):
-                for i in hidden_blocks:
-                    nc.tensor.matmul(
-                        h_ps[i][:],
-                        w_enc_sb[:, k, i * P : (i + 1) * P],
-                        y_sb[q][:, k, :],
-                        start=(k == 0),
-                        stop=(k == D_BLOCKS - 1),
-                    )
-            for i in hidden_blocks:
-                copy_out = nc.scalar.copy if i == 0 else second_copier(q)
-                copy_out(h_sb[q][:, i, :], h_ps[i][:])
+            z_ps = [[psum.tile([P, STEP], F32, tag="bank", name=f"z_ps{c}") for c in range(C_BLOCKS)] for s in range(STEPS)]
+            squares = [ring.tile([P, C_BLOCKS, STEP], F32, name="squares") for s in range(STEPS)]
+            for s in range(STEPS):
+                for c in range(C_BLOCKS):
+                    for i in range(H_BLOCKS):
+                        nc.tensor.matmul(
+                            z_ps[s][c][:],
+                            w_proj_sb[:, i, c * P : (c + 1) * P],
+                            h_sb[q][:, i, columns[s]],
+                            start=(i == 0),
+                            stop=(i == H_BLOCKS - 1),
+                        )
+                    nc.scalar.activation(squares[s][:, c, :], z_ps[s][c][:], FUNC.Square)
 
-        def project(q):
-            z_ps[q] = [psum.tile([P, BANK], F32, tag="bank", name=f"z_ps{c}") for c in range(C_BLOCKS)]
-            for i in range(H_BLOCKS):
+            sum_ps = [psum.tile([P, STEP], F32, tag="bank", name="sum_ps") for s in range(STEPS)]
+            for s in range(STEPS):
                 for c in range(C_BLOCKS):
                     nc.tensor.matmul(
-                        z_ps[q][c][:],
-                        w_proj_sb[:, i, c * P : (c + 1) * P],
-                        h_sb[q][:, i, :],
-                        start=(i == 0),
-                        stop=(i == H_BLOCKS - 1),
+                        sum_ps[s][:], ones[:], squares[s][:, c, :], start=(c == 0), stop=(c == C_BLOCKS - 1)
                     )
-            squares[q] = blocks.tile([P, C_BLOCKS, BANK], F32, name="squares")
-            for c in range(C_BLOCKS):
-                nc.scalar.activation(squares[q][:, c, :], z_ps[q][c][:], FUNC.Square)
+            for s in range(STEPS):
+                second_copier(z_sb[q][0][:, columns[s]], z_ps[s][0][:])
+            for s in range(STEPS):
+                nc.scalar.activation(r_sb[q][:, columns[s]], sum_ps[s][:], FUNC.Abs_reciprocal_sqrt)
+                second_copier(z_sb[q][1][:, columns[s]], z_ps[s][1][:])
 
-        def norm(q):
-            sum_ps = psum.tile([P, BANK], F32, tag="bank")
-            for c in range(C_BLOCKS):
-                nc.tensor.matmul(sum_ps[:], ones[:], squares[q][:, c, :], start=(c == 0), stop=(c == C_BLOCKS - 1))
-            second_copier(q)(z_sb[q][0][:], z_ps[q][0][:])
-            nc.scalar.activation(r_sb[q][:], sum_ps[:], FUNC.Abs_reciprocal_sqrt)
-            second_copier(q)(z_sb[q][1][:], z_ps[q][1][:])
-
-        def place(q):
             listed = offsets[:, q * LIST_COLUMNS : (q + 1) * LIST_COLUMNS]
             for c in range(C_BLOCKS):
                 nc.vector.tensor_tensor(window[c][:].indirect(listed), z_sb[q][c][:], r_sb[q][:], MULT)
-
-        encode(0, (0, 1))
-        for q in range(N_BLOCKS):
-            project(q)
-            if q + 1 < N_BLOCKS:
-                encode(q + 1, (0,))
-            norm(q)
-            if q + 1 < N_BLOCKS:
-                encode(q + 1, (1,))
-            place(q)
 
         for c in range(C_BLOCKS):
             nc.sync.dma_start(out[c * P : (c + 1) * P, :], window[c][:])

@@ -31,42 +31,50 @@ def tile_momentumcontrast_s_kernel(tc, base, y1, w_enc, w_proj, offs, out):
         w_proj_sb = held.tile([P, H_BLOCKS, C], BF16, name="w_proj_sb")
         window = [held.tile([P, S], F32, name=f"window{c}") for c in range(C_BLOCKS)]
         ones = held.tile([P, P], F32, name="ones")
-        y_sb = [held.tile([P, D_BLOCKS, PIECE], BF16, name=f"y{q}") for q in range(PIECES)]
+        y_sb = [held.tile([P, D_BLOCKS, N // 2], BF16, name=f"y{half}") for half in range(2)]
         h_sb = [held.tile([P, H_BLOCKS, PIECE], BF16, name=f"h{q}") for q in range(PIECES)]
-        z_sb = [[held.tile([P, PIECE], F32, name=f"z{q}_{c}") for c in range(C_BLOCKS)] for q in range(PIECES)]
-        r_sb = [held.tile([P, PIECE], F32, name=f"r{q}") for q in range(PIECES)]
+        z_sb = [held.tile([P, N], F32, name=f"z{c}") for c in range(C_BLOCKS)]
+        r_sb = held.tile([P, N], F32, name="r_sb")
 
-        y_view = y1.rearrange("(k p) n -> p k n", p=P)
-        nc.sync.dma_start(w_enc_sb[:], w_enc.rearrange("(k p) i -> p k i", p=P))
-        nc.scalar.dma_start(y_sb[0][:, :, 0:STEP], y_view[:, :, 0:STEP])
-        nc.sync.dma_start(y_sb[0][:, :, STEP:PIECE], y_view[:, :, STEP:PIECE])
+        y_view = y1.rearrange("(p k) n -> p k n", k=D_BLOCKS)
+        nc.sync.dma_start(w_enc_sb[:], w_enc.rearrange("(p k) i -> p k i", k=D_BLOCKS))
+        for k in range(D_BLOCKS):
+            queue = nc.scalar if k % 2 == 0 else nc.sync
+            queue.dma_start(y_sb[0][:, k, :], y_view[:, k, 0 : N // 2])
         nc.scalar.dma_start(w_proj_sb[:], w_proj.rearrange("(k p) c -> p k c", p=P))
-        nc.sync.dma_start(y_sb[1][:], y_view[:, :, PIECE : 2 * PIECE])
         nc.sync.dma_start(window[0][:], base[0:P, :])
         nc.sync.dma_start(offsets[:], offs)
         nc.sync.dma_start(window[1][:], base[P : 2 * P, :])
-        for q in range(2, PIECES):
-            nc.sync.dma_start(y_sb[q][:], y_view[:, :, q * PIECE : (q + 1) * PIECE])
+        nc.sync.dma_start(y_sb[1][:], y_view[:, :, N // 2 : N])
 
         nc.vector.memset(ones[:], 1.0)
+
+        def place(c, first, pieces):
+            listed = offsets[:, first * LIST_COLUMNS : (first + pieces) * LIST_COLUMNS]
+            samples = slice(first * PIECE, (first + pieces) * PIECE)
+            nc.vector.tensor_tensor(window[c][:].indirect(listed), z_sb[c][:, samples], r_sb[:, samples], MULT)
 
         for q in range(PIECES):
             second_copier = nc.vector.tensor_copy if q == 0 else nc.scalar.copy
             columns = [slice(s * STEP, (s + 1) * STEP) for s in range(STEPS)]
+            samples = [slice(q * PIECE + s * STEP, q * PIECE + (s + 1) * STEP) for s in range(STEPS)]
+            half_columns = [slice(sl.start % (N // 2), sl.start % (N // 2) + STEP) for sl in samples]
 
-            for s in range(STEPS):
-                for i in range(H_BLOCKS):
-                    h_ps = psum.tile([P, STEP], F32, tag="bank")
-                    for k in range(D_BLOCKS):
+            groups = [(s, i) for s in range(STEPS) for i in range(H_BLOCKS)]
+            for together in [groups] if q == 0 else [[group] for group in groups]:
+                h_ps = {group: psum.tile([P, STEP], F32, tag="bank", name="h_ps") for group in together}
+                for k in range(D_BLOCKS):
+                    for s, i in together:
                         nc.tensor.matmul(
-                            h_ps[:],
+                            h_ps[(s, i)][:],
                             w_enc_sb[:, k, i * P : (i + 1) * P],
-                            y_sb[q][:, k, columns[s]],
+                            y_sb[q // 2][:, k, half_columns[s]],
                             start=(k == 0),
                             stop=(k == D_BLOCKS - 1),
                         )
+                for s, i in together:
                     copy_out = nc.scalar.copy if i == 0 else second_copier
-                    copy_out(h_sb[q][:, i, columns[s]], h_ps[:])
+                    copy_out(h_sb[q][:, i, columns[s]], h_ps[(s, i)][:])
 
             z_ps = [[psum.tile([P, STEP], F32, tag="bank", name=f"z_ps{c}") for c in range(C_BLOCKS)] for s in range(STEPS)]
             squares = [ring.tile([P, C_BLOCKS, STEP], F32, name="squares") for s in range(STEPS)]
@@ -89,14 +97,16 @@ def tile_momentumcontrast_s_kernel(tc, base, y1, w_enc, w_proj, offs, out):
                         sum_ps[s][:], ones[:], squares[s][:, c, :], start=(c == 0), stop=(c == C_BLOCKS - 1)
                     )
             for s in range(STEPS):
-                second_copier(z_sb[q][0][:, columns[s]], z_ps[s][0][:])
+                second_copier(z_sb[0][:, samples[s]], z_ps[s][0][:])
             for s in range(STEPS):
-                nc.scalar.activation(r_sb[q][:, columns[s]], sum_ps[s][:], FUNC.Abs_reciprocal_sqrt)
-                second_copier(z_sb[q][1][:, columns[s]], z_ps[s][1][:])
+                nc.scalar.activation(r_sb[:, samples[s]], sum_ps[s][:], FUNC.Abs_reciprocal_sqrt)
+                second_copier(z_sb[1][:, samples[s]], z_ps[s][1][:])
 
-            listed = offsets[:, q * LIST_COLUMNS : (q + 1) * LIST_COLUMNS]
-            for c in range(C_BLOCKS):
-                nc.vector.tensor_tensor(window[c][:].indirect(listed), z_sb[q][c][:], r_sb[q][:], MULT)
-
-        for c in range(C_BLOCKS):
-            nc.sync.dma_start(out[c * P : (c + 1) * P, :], window[c][:])
+            if q < PIECES - 2:
+                place(0, q, 1)
+                place(1, q, 1)
+            else:
+                place(0, q, 1)
+        nc.sync.dma_start(out[0:P, :], window[0][:])
+        place(1, PIECES - 2, 2)
+        nc.sync.dma_start(out[P : 2 * P, :], window[1][:])

@@ -102,11 +102,8 @@ def tile_momentumcontrast_s_kernel(tc, base, y1, w_enc, w_proj, offs, out):
                 nc.scalar.activation(r_sb[:, samples[s]], sum_ps[s][:], FUNC.Abs_reciprocal_sqrt)
                 second_copier(z_sb[1][:, samples[s]], z_ps[s][1][:])
 
-            if q < PIECES - 2:
-                place(0, q, 1)
-                place(1, q, 1)
-            else:
-                place(0, q, 1)
-        nc.sync.dma_start(out[0:P, :], window[0][:])
-        place(1, PIECES - 2, 2)
-        nc.sync.dma_start(out[P : 2 * P, :], window[1][:])
+            for c in range(C_BLOCKS):
+                place(c, q, 1)
+
+        for c in range(C_BLOCKS):
+            nc.sync.dma_start(out[c * P : (c + 1) * P, :], window[c][:])

@@ -39,9 +39,9 @@ def tile_momentumcontrast_s_kernel(tc, base, y1, w_enc, w_proj, offs, out):
         y_view = y1.rearrange("(p k) n -> p k n", k=D_BLOCKS)
         nc.sync.dma_start(w_enc_sb[:], w_enc.rearrange("(p k) i -> p k i", k=D_BLOCKS))
         for k in range(D_BLOCKS):
-            queue = nc.scalar if k % 2 == 0 else nc.sync
+            queue = nc.scalar if k == 0 else nc.sync
             queue.dma_start(y_sb[0][:, k, :], y_view[:, k, 0 : N // 2])
-        nc.scalar.dma_start(w_proj_sb[:], w_proj.rearrange("(k p) c -> p k c", p=P))
+        nc.sync.dma_start(w_proj_sb[:], w_proj.rearrange("(k p) c -> p k c", p=P))
         nc.sync.dma_start(window[0][:], base[0:P, :])
         nc.sync.dma_start(offsets[:], offs)
         nc.sync.dma_start(window[1][:], base[P : 2 * P, :])

@@ -45,7 +45,10 @@ def tile_momentumcontrast_s_kernel(tc, base, y1, w_enc, w_proj, offs, out):
         nc.sync.dma_start(window[0][:], base[0:P, :])
         nc.sync.dma_start(offsets[:], offs)
         nc.sync.dma_start(window[1][:], base[P : 2 * P, :])
-        nc.sync.dma_start(y_sb[1][:], y_view[:, :, N // 2 : N])
+        for q in range(PIECES // 2, PIECES):
+            nc.sync.dma_start(
+                y_sb[1][:, :, q * PIECE - N // 2 : (q + 1) * PIECE - N // 2], y_view[:, :, q * PIECE : (q + 1) * PIECE]
+            )
 
         nc.vector.memset(ones[:], 1.0)
 

@@ -105,8 +105,11 @@ def tile_momentumcontrast_s_kernel(tc, base, y1, w_enc, w_proj, offs, out):
                 nc.scalar.activation(r_sb[:, samples[s]], sum_ps[s][:], FUNC.Abs_reciprocal_sqrt)
                 second_copier(z_sb[1][:, samples[s]], z_ps[s][1][:])
 
-            for c in range(C_BLOCKS):
-                place(c, q, 1)
-
-        for c in range(C_BLOCKS):
-            nc.sync.dma_start(out[c * P : (c + 1) * P, :], window[c][:])
+            if q < PIECES - 2:
+                place(0, q, 1)
+                place(1, q, 1)
+            else:
+                place(0, q, 1)
+        nc.sync.dma_start(out[0:P, :], window[0][:])
+        place(1, PIECES - 2, 2)
+        nc.sync.dma_start(out[P : 2 * P, :], window[1][:])

import concourse.mybir as mybir

F32 = mybir.dt.float32
BF16 = mybir.dt.bfloat16
U16 = mybir.dt.uint16
FUNC = mybir.ActivationFunctionType
MULT = mybir.AluOpType.mult

P = 128
D, H, C, S, N = 512, 256, 256, 4096, 2048
D_BLOCKS, H_BLOCKS, C_BLOCKS = D // P, H // P, C // P
PIECE = 512
PIECES = N // PIECE
STEPS = 2
STEP = PIECE // STEPS
LIST_COLUMNS = PIECE // 16
PSUM_BANKS = 8

FLOPS = 2 * N * (D * H + H * C + C)


def tile_momentumcontrast_s_kernel(tc, base, y1, w_enc, w_proj, offs, out):
    nc = tc.nc
    with (
        tc.tile_pool(name="held", bufs=1) as held,
        tc.tile_pool(name="ring", bufs=2 * STEPS) as ring,
        tc.psum_pool(name="psum", bufs=PSUM_BANKS) as psum,
    ):
        offsets = held.tile([P, N // 16], U16, name="offsets")
        w_enc_sb = held.tile([P, D_BLOCKS, H], BF16, name="w_enc_sb")
        w_proj_sb = held.tile([P, H_BLOCKS, C], BF16, name="w_proj_sb")
        window = [held.tile([P, S], F32, name=f"window{c}") for c in range(C_BLOCKS)]
        ones = held.tile([P, P], F32, name="ones")
        y_sb = [held.tile([P, D_BLOCKS, N // 2], BF16, name=f"y{half}") for half in range(2)]
        h_sb = [held.tile([P, H_BLOCKS, PIECE], BF16, name=f"h{q}") for q in range(PIECES)]
        z_sb = [held.tile([P, N], F32, name=f"z{c}") for c in range(C_BLOCKS)]
        r_sb = held.tile([P, N], F32, name="r_sb")

        y_view = y1.rearrange("(p k) n -> p k n", k=D_BLOCKS)
        nc.sync.dma_start(w_enc_sb[:], w_enc.rearrange("(p k) i -> p k i", k=D_BLOCKS))
        for k in range(D_BLOCKS):
            queue = nc.scalar if k == 0 else nc.sync
            queue.dma_start(y_sb[0][:, k, :], y_view[:, k, 0 : N // 2])
        nc.sync.dma_start(w_proj_sb[:], w_proj.rearrange("(k p) c -> p k c", p=P))
        nc.sync.dma_start(window[0][:], base[0:P, :])
        nc.sync.dma_start(offsets[:], offs)
        nc.sync.dma_start(window[1][:], base[P : 2 * P, :])
        for q in range(PIECES // 2, PIECES):
            nc.sync.dma_start(
                y_sb[1][:, :, q * PIECE - N // 2 : (q + 1) * PIECE - N // 2], y_view[:, :, q * PIECE : (q + 1) * PIECE]
            )

        nc.vector.memset(ones[:], 1.0)

        def place(c, first, pieces):
            listed = offsets[:, first * LIST_COLUMNS : (first + pieces) * LIST_COLUMNS]
            samples = slice(first * PIECE, (first + pieces) * PIECE)
            nc.vector.tensor_tensor(window[c][:].indirect(listed), z_sb[c][:, samples], r_sb[:, samples], MULT)

        for q in range(PIECES):
            second_copier = nc.vector.tensor_copy if q == 0 else nc.scalar.copy
            columns = [slice(s * STEP, (s + 1) * STEP) for s in range(STEPS)]
            samples = [slice(q * PIECE + s * STEP, q * PIECE + (s + 1) * STEP) for s in range(STEPS)]
            half_columns = [slice(sl.start % (N // 2), sl.start % (N // 2) + STEP) for sl in samples]

            groups = [(s, i) for s in range(STEPS) for i in range(H_BLOCKS)]
            for together in [groups] if q == 0 else [[group] for group in groups]:
                h_ps = {group: psum.tile([P, STEP], F32, tag="bank", name="h_ps") for group in together}
                for k in range(D_BLOCKS):
                    for s, i in together:
                        nc.tensor.matmul(
                            h_ps[(s, i)][:],
                            w_enc_sb[:, k, i * P : (i + 1) * P],
                            y_sb[q // 2][:, k, half_columns[s]],
                            start=(k == 0),
                            stop=(k == D_BLOCKS - 1),
                        )
                for s, i in together:
                    copy_out = nc.scalar.copy if i == 0 else second_copier
                    copy_out(h_sb[q][:, i, columns[s]], h_ps[(s, i)][:])

            z_ps = [[psum.tile([P, STEP], F32, tag="bank", name=f"z_ps{c}") for c in range(C_BLOCKS)] for s in range(STEPS)]
            squares = [ring.tile([P, C_BLOCKS, STEP], F32, name="squares") for s in range(STEPS)]
            for s in range(STEPS):
                for c in range(C_BLOCKS):
                    for i in range(H_BLOCKS):
                        nc.tensor.matmul(
                            z_ps[s][c][:],
                            w_proj_sb[:, i, c * P : (c + 1) * P],
                            h_sb[q][:, i, columns[s]],
                            start=(i == 0),
                            stop=(i == H_BLOCKS - 1),
                        )
                    nc.scalar.activation(squares[s][:, c, :], z_ps[s][c][:], FUNC.Square)

            sum_ps = [psum.tile([P, STEP], F32, tag="bank", name="sum_ps") for s in range(STEPS)]
            for s in range(STEPS):
                for c in range(C_BLOCKS):
                    nc.tensor.matmul(
                        sum_ps[s][:], ones[:], squares[s][:, c, :], start=(c == 0), stop=(c == C_BLOCKS - 1)
                    )
            for s in range(STEPS):
                second_copier(z_sb[0][:, samples[s]], z_ps[s][0][:])
            for s in range(STEPS):
                nc.scalar.activation(r_sb[:, samples[s]], sum_ps[s][:], FUNC.Abs_reciprocal_sqrt)
                second_copier(z_sb[1][:, samples[s]], z_ps[s][1][:])

            if q < PIECES - 2:
                place(0, q, 1)
                place(1, q, 1)
            else:
                place(0, q, 1)
        nc.sync.dma_start(out[0:P, :], window[0][:])
        place(1, PIECES - 2, 2)
        nc.sync.dma_start(out[P : 2 * P, :], window[1][:])
